import numpy as np
import ml_dtypes


def mxq(x, axis, fmt="e4m3"):
    dtype, down = {"e4m3": (ml_dtypes.float8_e4m3fn, 7), "e5m2": (ml_dtypes.float8_e5m2, 14)}[fmt]
    v = np.moveaxis(np.asarray(x, np.float32).astype(ml_dtypes.bfloat16).astype(np.float64), axis, -1)
    blocks = v.reshape(v.shape[:-1] + (-1, 32))
    amax = np.abs(blocks).max(-1, keepdims=True)
    byte = np.maximum(np.where(amax > 0, np.frexp(amax)[1] - 1 + 127, 0) - down, 1)
    scale = np.exp2(byte - 127.0)
    codes = (blocks / scale).astype(np.float32).astype(dtype).astype(np.float64)
    return np.moveaxis((codes * scale).reshape(v.shape), -1, axis)


WIDE = False


def mx_kscale(k):
    if not WIDE:
        return np.ones(k)
    levels = np.array([10, -10, 5, -5, 0])
    if k % 512:
        return np.exp2(np.random.permutation(np.resize(levels, k // 32))).repeat(32)
    a = np.empty((k // 512, 16))
    for p in range(k // 512):
        a[p, :8] = np.random.permutation(np.resize(levels, 8))
        for g in range(8):
            far = levels[np.abs(levels - a[p, g]) >= 10]
            a[p, g + 8] = far[np.random.randint(len(far))]
    return np.exp2(a.ravel()).repeat(32)


BF16 = ml_dtypes.bfloat16


def bf(x):
    return np.asarray(x, np.float32).astype(BF16)


def f64(x):
    return np.asarray(x).astype(np.float64)


B, S, DIM, HDIM = 2, 256, 1024, 4096


def draw0():
    s = mx_kscale(DIM)
    t = np.exp2(np.round(np.log2(mx_kscale(HDIM)) / 2))
    return {"x": bf(np.random.standard_normal((B, S, DIM)) * s),
            "W1": bf(np.random.standard_normal((HDIM, DIM)) * (1.0 / np.sqrt(DIM)) / s[None, :] * t[:, None]),
            "W2": bf(np.random.standard_normal((HDIM, DIM)) * (1.0 / np.sqrt(HDIM)) / (t * t)[:, None])}


def core(x, W1, W2):
    pre = mxq(f64(x), 2, "e4m3") @ mxq(f64(W1), 1, "e4m3").T
    post = np.square(np.maximum(pre, 0.0))
    out = mxq(post, 2, "e4m3") @ mxq(f64(W2), 0, "e4m3")
    return out


def e4m3fn_bytes(y):
    return np.clip(np.asarray(y, np.float64), -448.0, 448.0).astype(np.float32).astype(ml_dtypes.float8_e4m3fn).view(np.uint8)


def e4m3fn_values(b):
    return np.asarray(b, np.uint8).view(ml_dtypes.float8_e4m3fn).astype(np.float64)


def setup_inputs():
    d = draw0()
    x0 = np.asarray(d['W2']).astype(np.float64)
    s = (np.max(np.abs(x0), axis=(1,), keepdims=True) / 448.0).astype(np.float32)
    out = {}
    for k, v in d.items():
        if k == 'W2':
            out['W2_bytes'] = e4m3fn_bytes(x0 / s.astype(np.float64))
            out['W2_scale'] = s
        else:
            out[k] = v
    return out


def reference(x, W1, W2_bytes, W2_scale):
    return core(x, W1, e4m3fn_values(W2_bytes) * W2_scale.astype(np.float64))

@@ -1,0 +1,408 @@
+from contextlib import ExitStack
+
+import concourse.mybir as mybir
+from concourse.masks import make_identity
+
+TOK, DIM, HID = 512, 1024, 4096
+FLOPS = 2 * 2 * TOK * DIM * HID
+
+F32 = mybir.dt.float32
+BF16 = mybir.dt.bfloat16
+U32 = mybir.dt.uint32
+U8 = mybir.dt.uint8
+FP8 = mybir.dt.float8_e4m3fn
+FP8X4 = mybir.dt.float8_e4m3fn_x4
+AF = mybir.ActivationFunctionType
+ALU = mybir.AluOpType
+
+P = 128
+N_PAIRS = 16
+N_PASS = 8
+DUMMIES = 8
+LEAD = [2,0,2,0,2,1,2,0,2,1,1,1,0,0,0,0]
+HEAD_PAIRS = 2
+W2_HEAD = [3,0,1,3]
+W2_SLOT = [2,5,1,5,7,2,4,7,2,3,3,1,4,3,5,2]
+W2_TAIL = 1
+ON_SCALAR = [(4, 2)]
+LATE = []
+LATE_FIRST = 0
+LOADS = ["v0","x0","x1","v1","x2","x3","v2","p0","v3","p1","w10","p2","p3","p4","w11","p5","w20","w21"]
+MM_SLOT = [4,2,5,6,5,8,2,4,4,5,4,4,6,5,5,7]
+O_BUFS = 8
+W1C_BUFS = 10
+SQ_LAG = 2
+
+
+def tile_mlp_kernel(tc, x, W1, W2_bytes, W2_scale, out):
+    nc = tc.nc
+    x_v = x.rearrange("b s k -> (b s) k").rearrange("(p i) k -> p i k", i=4)
+    w1_v = W1.rearrange("(a m t) k -> a m t k", m=P, t=4)
+    w2_v = W2_bytes.rearrange("(a p t) d -> a p t d", p=P, t=4)
+    sc_v = W2_scale.rearrange("(a p t) o -> p a (t o)", p=P, t=4)
+    out_v = out.rearrange("b s d -> (b s) d").rearrange("(p i) d -> p i d", i=4)
+
+    with ExitStack() as ctx:
+        keep = ctx.enter_context(tc.tile_pool(name="keep", bufs=1))
+        work = ctx.enter_context(tc.tile_pool(name="work", bufs=2))
+        psum = ctx.enter_context(tc.psum_pool(name="psum", bufs=1))
+
+        ident = keep.tile([P, P], F32, name="ident")
+        zeros = keep.tile([P, 512], BF16, name="zeros")
+        probe = keep.tile([P, 1], F32, name="probe")
+        probe2 = keep.tile([P, 1], F32, name="probe2")
+        scale = keep.tile([P, N_PASS, 4], F32, name="scale")
+        xg = [keep.tile([P, 2048], BF16, name="xg%d" % n, align_bytes=64) for n in range(2)]
+        xc = keep.tile([P, 1024], U32, name="xc", align_bytes=64)
+        xs = keep.tile([P, 1024], U8, name="xs", align_bytes=64)
+
+        ctx.enter_context(tc.manual_schedule())
+
+        raw = {}
+        bytes_t = {}
+        wide = {}
+        w2g = {}
+        w2c = {}
+        w2s = {}
+        wg = {}
+        w1c = {}
+        w1s = {}
+        rel = {}
+        pg = {}
+        pc = {}
+        ps = {}
+        tp = {}
+        p1 = {}
+        acc = {}
+        n_unit = [0]
+
+        def bank(tag):
+            return psum.tile([P, 512], F32, name="bk_" + tag, tag=tag)
+
+        def load_x(i):
+            raw["x", i] = work.tile([P, 1024], BF16, name="xraw", tag="xraw", bufs=4)
+            nc.sync.dma_start(out=raw["x", i][:], in_=x_v[:, i, :])
+
+        def load_w1(j):
+            t = work.tile([P, 2, 1024], BF16, name="w1raw", tag="w1raw", bufs=6)
+            nc.sync.dma_start(out=t[:], in_=w1_v[j // 2][:, 2 * (j % 2) : 2 * (j % 2) + 2, :])
+            raw["w", 2 * j] = t[:, 0, :]
+            raw["w", 2 * j + 1] = t[:, 1, :]
+
+        def load_w2(q, h):
+            t = work.tile([P, 2, 1024], U8, name="w2b", tag="w2b", bufs=6)
+            nc.sync.dma_start(out=t[:], in_=w2_v[q][:, 2 * h : 2 * h + 2, :])
+            bytes_t[q, 2 * h] = t[:, 0, :]
+            bytes_t[q, 2 * h + 1] = t[:, 1, :]
+
+        def load_w2_row(q, t):
+            b = keep.tile([P, 1024], U8, name="w2r%d" % t)
+            nc.sync.dma_start(out=b[:], in_=w2_v[q][:, t, :])
+            bytes_t[q, t] = b[:]
+
+        def transposes(kind, n, b):
+            src = raw[kind, n]
+            words = (src[:] if kind == "x" else src).bitcast(F32)
+            t = bank("tp%d" % b)
+            tp[kind, n] = t
+            for g in range(2):
+                for u in range(2):
+                    nc.tensor.transpose(
+                        t[:, (2 * g + u) * P : (2 * g + u + 1) * P],
+                        words[:, 256 * g + u : 256 * (g + 1) : 2],
+                        ident[:],
+                    )
+
+        def evac(kind, n):
+            src = tp[kind, n][:].rearrange("p (g u m) -> p g m u", g=2, u=2)
+            if kind == "x":
+                dst = xg[n // 2][:].bitcast(F32).rearrange("p (g i m u) -> p g i m u", g=2, i=2, u=2)[:, :, n % 2]
+            else:
+                if n % 2 == 0:
+                    wg[n // 2] = work.tile([P, 2048], BF16, name="wg", tag="wg", bufs=4, align_bytes=64)
+                h = n % 2
+                dst = wg[n // 2][:, h * 1024 : (h + 1) * 1024].bitcast(F32).rearrange("p (g m u) -> p g m u", g=2, u=2)
+            nc.scalar.copy(out=dst, in_=src)
+
+        def quant_x(ip, g):
+            o = slice(g * 512 + ip * 256, g * 512 + ip * 256 + 256)
+            nc.vector.quantize_mx(
+                out=xc[:, o].bitcast(FP8X4), scales=xs[:, o],
+                in_=xg[ip][:, g * 1024 : (g + 1) * 1024],
+            )
+
+        def quant_w1(j):
+            w1c[j] = work.tile([P, 512], U32, name="w1c", tag="w1c", bufs=W1C_BUFS, align_bytes=64)
+            w1s[j] = work.tile([P, 512], U8, name="w1s", tag="w1s", bufs=W1C_BUFS, align_bytes=64)
+            nc.vector.quantize_mx(out=w1c[j][:].bitcast(FP8X4), scales=w1s[j][:], in_=wg[j][:])
+
+        def mm1(m, h):
+            t = bank("p1%d" % (n_unit[0] % 2))
+            n_unit[0] += 1
+            p1[m, h] = t
+            for s in range(2):
+                for g in range(2):
+                    c = slice((2 * s + g) * P, (2 * s + g + 1) * P)
+                    r = slice(g * 512 + h * 256, g * 512 + h * 256 + 256)
+                    nc.tensor.matmul_mx(
+                        out=t[:, s * 256 : (s + 1) * 256], lhsT=w1c[m][:, c].bitcast(FP8X4), lhsT_scale=w1s[m][:, c],
+                        rhs=xc[:, r].bitcast(FP8X4), rhs_scale=xs[:, r], start=(g == 0), stop=(g == 1),
+                    )
+
+        def relu(m, h):
+            q, t = m // 2, 2 * (m % 2)
+            if t == 0 and h == 0:
+                rel[q] = work.tile([P, 4, 512], F32, name="rel", tag="rel", bufs=2)
+            nc.scalar.activation(
+                out=rel[q][:, t : t + 2, h * 256 : (h + 1) * 256],
+                in_=p1[m, h][:].rearrange("p (t n) -> p t n", t=2), func=AF.Relu,
+            )
+
+        def square(q, h):
+            pg[q, h] = work.tile([P, 1024], BF16, name="pg", tag="pg", bufs=4, align_bytes=64)
+            nc.scalar.activation(
+                out=pg[q, h][:].rearrange("p (c i t) -> p c t i", i=4, t=4),
+                in_=rel[q][:, :, h * 256 : (h + 1) * 256].rearrange("p t (c i) -> p c t i", i=4),
+                func=AF.Square,
+            )
+
+        def quant_post(q, h):
+            if h == 0:
+                pc[q] = keep.tile([P, 512], U32, name="pc%d" % q, align_bytes=64)
+                ps[q] = keep.tile([P, 512], U8, name="ps%d" % q, align_bytes=64)
+            o = slice(h * 256, (h + 1) * 256)
+            nc.vector.quantize_mx(out=pc[q][:, o].bitcast(FP8X4), scales=ps[q][:, o], in_=pg[q, h][:])
+
+        def widen(q, t):
+            if q not in wide:
+                wide[q] = work.tile([P, 4, 1024], BF16, name="wide", tag="wide", bufs=2)
+            src = bytes_t[q, t].bitcast(FP8)
+            if (q, t) in ON_SCALAR or (q == N_PASS - 1 and t in LATE):
+                nc.scalar.activation(out=wide[q][:, t, :], in_=src, func=AF.Copy, scale=scale[:, q, t : t + 1])
+            else:
+                nc.vector.tensor_scalar(
+                    out=wide[q][:, t, :], in0=src, scalar1=scale[:, q, t : t + 1], scalar2=None, op0=ALU.mult
+                )
+
+        def interleave(q, h):
+            w2g[q, h] = work.tile([P, 2048], BF16, name="w2g", tag="w2g", bufs=3, align_bytes=64)
+            nc.vector.tensor_copy(
+                out=w2g[q, h][:].rearrange("p (c i t) -> p c t i", i=4, t=4),
+                in_=wide[q][:, :, h * 512 : (h + 1) * 512].rearrange("p t (c i) -> p c t i", i=4),
+            )
+
+        def quant_w2(q, h):
+            if h == 0:
+                w2c[q] = keep.tile([P, 1024], U32, name="w2c%d" % q, align_bytes=64)
+                w2s[q] = keep.tile([P, 1024], U8, name="w2s%d" % q, align_bytes=64)
+            o = slice(h * 512, (h + 1) * 512)
+            nc.vector.quantize_mx(out=w2c[q][:, o].bitcast(FP8X4), scales=w2s[q][:, o], in_=w2g[q, h][:])
+
+        stream = [("widen", 0, t) for t in range(4)]
+        for q in range(N_PASS):
+            nxt = [("widen", q + 1, t) if q + 1 < N_PASS and not (q + 1 == N_PASS - 1 and t in LATE) else None for t in range(4)]
+            tail = [("interleave", q, 0), ("quant", q, 0), ("interleave", q, 1), ("quant", q, 1)]
+            for a, b in zip(nxt, tail):
+                if a:
+                    stream.append(a)
+                stream.append(b)
+        pos = [0]
+        cap = [stream.index(("interleave", N_PASS - 1, 0))]
+
+        def w2_work(n):
+            n = min(n, cap[0] - pos[0])
+            for kind, q, a in stream[pos[0] : pos[0] + n]:
+                if kind == "widen":
+                    widen(q, a)
+                    if a % 2 == 1 and q + 3 < N_PASS:
+                        load_w2(q + 3, a // 2)
+                elif kind == "interleave":
+                    interleave(q, a)
+                else:
+                    quant_w2(q, a)
+            pos[0] += n
+
+        tags = {(0, 1): "tp0", (1, 1): "tp1", (2, 1): "p10", (3, 1): "p11"}
+
+        def mm2(i, half, q):
+            if q == 0:
+                acc[i, half] = bank(tags.get((i, half), "acc%d" % i))
+            c = slice(i * P, (i + 1) * P)
+            r = slice(half * 512, (half + 1) * 512)
+            nc.tensor.matmul_mx(
+                out=acc[i, half][:], lhsT=pc[q][:, c].bitcast(FP8X4), lhsT_scale=ps[q][:, c],
+                rhs=w2c[q][:, r].bitcast(FP8X4), rhs_scale=w2s[q][:, r],
+                start=(q == 0), stop=(q == N_PASS - 1),
+            )
+
+        def finish(i, half, on_scalar):
+            o = work.tile([P, 512], F32, name="o", tag="o", bufs=O_BUFS)
+            if on_scalar:
+                nc.scalar.copy(out=o[:], in_=acc[i, half][:])
+            else:
+                nc.vector.tensor_copy(out=o[:], in_=acc[i, half][:])
+            nc.sync.dma_start(out=out_v[:, i, half * 512 : (half + 1) * 512], in_=o[:])
+
+        nc.vector.memset(zeros[:], 0.0)
+        nc.vector.memset(probe[:], 0.0)
+        make_identity(nc, ident[:])
+        nc.scalar.dma_start(out=scale[:], in_=sc_v)
+        nc.scalar.activation(out=probe2[:], in_=probe[:], func=AF.Square)
+        for code in LOADS:
+            if code[0] == "x":
+                load_x(int(code[1]))
+            elif code[0] == "p":
+                load_w1(int(code[1]))
+            elif code[0] == "v":
+                load_w2_row(0, int(code[1]))
+            else:
+                load_w2(int(code[1]), int(code[2]))
+
+        warm = bank("acc3")
+        for d in range(DUMMIES):
+            nc.tensor.matmul(warm[:], lhsT=zeros[:, :P], rhs=zeros[:], start=True, stop=True)
+
+        w2_work(W2_HEAD[0])
+        for ip in range(2):
+            for i in (2 * ip, 2 * ip + 1):
+                transposes("x", i, i % 2)
+            for i in (2 * ip, 2 * ip + 1):
+                evac("x", i)
+            for g in range(2):
+                quant_x(ip, g)
+        w2_work(W2_HEAD[1])
+
+        n_t = [0]
+
+        def tpair():
+            j = n_t[0]
+            for s in range(2):
+                transposes("w", 2 * j + s, s)
+            if j + 6 < N_PAIRS:
+                load_w1(j + 6)
+            for s in range(2):
+                evac("w", 2 * j + s)
+            n_t[0] += 1
+            return j
+
+        for n in range(HEAD_PAIRS):
+            j = tpair()
+            w2_work(W2_HEAD[2 + n])
+            quant_w1(j)
+
+        units = []
+        for q in range(N_PASS):
+            if q < N_PASS - 1:
+                units += [(2 * q, 0), (2 * q, 1), (2 * q + 1, 0), (2 * q + 1, 1)]
+            else:
+                units += [(2 * q, 0), (2 * q + 1, 0), (2 * q, 1), (2 * q + 1, 1)]
+        squares = [(q, h) for q in range(N_PASS) for h in range(2)]
+        post_at = {}
+        w2_at = {}
+        nxt = {}
+        accs = [(0, 0), (1, 0), (2, 0), (3, 0), (0, 1), (1, 1), (2, 1), (3, 1)]
+
+        def picks(m, limit):
+            res = []
+            more = True
+            while more and len(res) < limit:
+                more = False
+                for a in accs:
+                    i, half = a
+                    q = nxt.get(a, 0)
+                    if q == N_PASS or len(res) == limit:
+                        continue
+                    if half == 1 and i < 2 and n_t[0] < N_PAIRS:
+                        continue
+                    if half == 1 and i >= 2 and m < N_PAIRS:
+                        continue
+                    if m > post_at.get((q, i // 2), 999) and m > w2_at.get((q, half), 999):
+                        res.append((i, half, q))
+                        nxt[a] = q + 1
+                        more = True
+            return res
+
+        order = []
+
+        def run_mm(lst):
+            for i, half, q in lst:
+                mm2(i, half, q)
+                if q == N_PASS - 1:
+                    order.append((i, half))
+
+        def w2_run(m, n):
+            n = min(n, cap[0] - pos[0])
+            for kind, q, a in stream[pos[0] : pos[0] + n]:
+                if kind == "quant":
+                    w2_at[q, a] = m
+            w2_work(n)
+
+        for kind, q, a in stream[: pos[0]]:
+            if kind == "quant":
+                w2_at[q, a] = -1
+
+        def post(m):
+            if 0 <= m - SQ_LAG - 1 < 2 * N_PASS:
+                k = squares[m - SQ_LAG - 1]
+                quant_post(*k)
+                post_at[k] = m
+
+        for m in range(N_PAIRS):
+            passes = picks(m, MM_SLOT[m])
+            ua, ub = units[2 * m], units[2 * m + 1]
+            n2 = W2_SLOT[m]
+            if LEAD[m]:
+                j = tpair()
+                w2_run(m, n2 // 2)
+                post(m)
+                quant_w1(j)
+                mm1(*ua)
+                mm1(*ub)
+                relu(*ua)
+                relu(*ub)
+                if LEAD[m] == 1:
+                    run_mm(passes)
+                for r in range(LEAD[m] - 1):
+                    j = tpair()
+                    if r == 0:
+                        w2_run(m, n2 - n2 // 2)
+                    quant_w1(j)
+                    if r == 0:
+                        run_mm(passes)
+                if LEAD[m] == 1:
+                    w2_run(m, n2 - n2 // 2)
+            else:
+                mm1(*ua)
+                run_mm(passes[:2])
+                mm1(*ub)
+                run_mm(passes[2:])
+                relu(*ua)
+                relu(*ub)
+                w2_run(m, 1)
+                post(m)
+                w2_run(m, n2 - 1)
+            if SQ_LAG <= m:
+                square(*squares[m - SQ_LAG])
+        rest = [squares[N_PAIRS - SQ_LAG + i] for i in range(SQ_LAG)]
+        m = N_PAIRS
+        cap[0] = len(stream) if LATE_FIRST >= len(LATE) else cap[0]
+        for t in LATE[:LATE_FIRST]:
+            widen(N_PASS - 1, t)
+        w2_run(m, W2_TAIL)
+        for n in range(SQ_LAG + 1):
+            if n < SQ_LAG:
+                square(*rest[n])
+                if n == 0:
+                    cap[0] = len(stream)
+                    for t in LATE[LATE_FIRST:]:
+                        widen(N_PASS - 1, t)
+            post(m)
+            run_mm(picks(m, 7))
+            w2_run(m, 2)
+            m += 1
+        w2_run(m, 60)
+        m += 1
+        run_mm(picks(m, 64))
+        assert len(order) == 8, nxt
+        for n, (i, half) in enumerate(order):
+            finish(i, half, n % 2 == 0)

@@ -19,17 +19,17 @@ P = 128
 N_PAIRS = 16
 N_PASS = 8
 DUMMIES = 8
-LEAD = [2,0,2,0,2,1,2,0,2,1,1,1,0,0,0,0]
+LEAD = [2,0,2,1,2,2,1,1,1,1,0,1,0,0,0,0]
 HEAD_PAIRS = 2
-W2_HEAD = [3,0,1,3]
-W2_SLOT = [2,5,1,5,7,2,4,7,2,3,3,1,4,3,5,2]
+W2_HEAD = [4,1,0,4]
+W2_SLOT = [2,2,6,5,4,4,5,2,1,4,2,4,3,2,3,5]
 W2_TAIL = 1
-ON_SCALAR = [(4, 2)]
+ON_SCALAR = []
 LATE = []
 LATE_FIRST = 0
-LOADS = ["v0","x0","x1","v1","x2","x3","v2","p0","v3","p1","w10","p2","p3","p4","w11","p5","w20","w21"]
-MM_SLOT = [4,2,5,6,5,8,2,4,4,5,4,4,6,5,5,7]
-O_BUFS = 8
+LOADS = ["x0","v0","x1","v2","v1","x2","x3","v3","p0","w10","p1","p2","w11","p3","p5","p4","w21","w20"]
+MM_SLOT = [1,6,5,3,8,1,2,3,5,6,3,8,6,4,5,4]
+REL_BUFS = 3
 W1C_BUFS = 10
 SQ_LAG = 2
 
@@ -152,7 +152,7 @@ def tile_mlp_kernel(tc, x, W1, W2_bytes, W2_scale, out):
         def relu(m, h):
             q, t = m // 2, 2 * (m % 2)
             if t == 0 and h == 0:
-                rel[q] = work.tile([P, 4, 512], F32, name="rel", tag="rel", bufs=2)
+                rel[q] = work.tile([P, 4, 512], F32, name="rel", tag="rel", bufs=REL_BUFS)
             nc.scalar.activation(
                 out=rel[q][:, t : t + 2, h * 256 : (h + 1) * 256],
                 in_=p1[m, h][:].rearrange("p (t n) -> p t n", t=2), func=AF.Relu,
@@ -175,21 +175,20 @@ def tile_mlp_kernel(tc, x, W1, W2_bytes, W2_scale, out):
 
         def widen(q, t):
             if q not in wide:
-                wide[q] = work.tile([P, 4, 1024], BF16, name="wide", tag="wide", bufs=2)
+                wide[q] = work.tile([P, 2, 1024, 2], BF16, name="wide", tag="wide", bufs=2)
             src = bytes_t[q, t].bitcast(FP8)
-            if (q, t) in ON_SCALAR or (q == N_PASS - 1 and t in LATE):
-                nc.scalar.activation(out=wide[q][:, t, :], in_=src, func=AF.Copy, scale=scale[:, q, t : t + 1])
-            else:
-                nc.vector.tensor_scalar(
-                    out=wide[q][:, t, :], in0=src, scalar1=scale[:, q, t : t + 1], scalar2=None, op0=ALU.mult
-                )
+            nc.vector.tensor_scalar(
+                out=wide[q][:, t // 2, :, t % 2], in0=src, scalar1=scale[:, q, t : t + 1], scalar2=None, op0=ALU.mult
+            )
 
         def interleave(q, h):
             w2g[q, h] = work.tile([P, 2048], BF16, name="w2g", tag="w2g", bufs=3, align_bytes=64)
-            nc.vector.tensor_copy(
-                out=w2g[q, h][:].rearrange("p (c i t) -> p c t i", i=4, t=4),
-                in_=wide[q][:, :, h * 512 : (h + 1) * 512].rearrange("p t (c i) -> p c t i", i=4),
-            )
+            dst = w2g[q, h][:].rearrange("p (n r e) -> p n r e", r=2, e=2)
+            src = wide[q][:, :, h * 512 : (h + 1) * 512, :].rearrange("p r n e -> p n r e")
+            if (q, h) in ON_SCALAR:
+                nc.scalar.copy(out=dst, in_=src)
+            else:
+                nc.vector.tensor_copy(out=dst, in_=src)
 
         def quant_w2(q, h):
             if h == 0:
@@ -198,9 +197,9 @@ def tile_mlp_kernel(tc, x, W1, W2_bytes, W2_scale, out):
             o = slice(h * 512, (h + 1) * 512)
             nc.vector.quantize_mx(out=w2c[q][:, o].bitcast(FP8X4), scales=w2s[q][:, o], in_=w2g[q, h][:])
 
-        stream = [("widen", 0, t) for t in range(4)]
+        stream = [("widen", 0, t) for t in (0, 2, 1, 3)]
         for q in range(N_PASS):
-            nxt = [("widen", q + 1, t) if q + 1 < N_PASS and not (q + 1 == N_PASS - 1 and t in LATE) else None for t in range(4)]
+            nxt = [("widen", q + 1, t) if q + 1 < N_PASS else None for t in (0, 2, 1, 3)]
             tail = [("interleave", q, 0), ("quant", q, 0), ("interleave", q, 1), ("quant", q, 1)]
             for a, b in zip(nxt, tail):
                 if a:
@@ -214,7 +213,7 @@ def tile_mlp_kernel(tc, x, W1, W2_bytes, W2_scale, out):
             for kind, q, a in stream[pos[0] : pos[0] + n]:
                 if kind == "widen":
                     widen(q, a)
-                    if a % 2 == 1 and q + 3 < N_PASS:
+                    if a in (1, 3) and q + 3 < N_PASS:
                         load_w2(q + 3, a // 2)
                 elif kind == "interleave":
                     interleave(q, a)
@@ -235,8 +234,9 @@ def tile_mlp_kernel(tc, x, W1, W2_bytes, W2_scale, out):
                 start=(q == 0), stop=(q == N_PASS - 1),
             )
 
-        def finish(i, half, on_scalar):
-            o = work.tile([P, 512], F32, name="o", tag="o", bufs=O_BUFS)
+        def finish(n, i, half, on_scalar):
+            tag, bufs = ("w1raw", 6) if n < 6 else ("wide", 2)
+            o = work.tile([P, 512], F32, name="o", tag=tag, bufs=bufs)
             if on_scalar:
                 nc.scalar.copy(out=o[:], in_=acc[i, half][:])
             else:
@@ -405,4 +405,4 @@ def tile_mlp_kernel(tc, x, W1, W2_bytes, W2_scale, out):
         run_mm(picks(m, 64))
         assert len(order) == 8, nxt
         for n, (i, half) in enumerate(order):
-            finish(i, half, n % 2 == 0)
+            finish(n, i, half, n % 2 == 0)

@@ -18,20 +18,26 @@ ALU = mybir.AluOpType
 P = 128
 N_PAIRS = 16
 N_PASS = 8
-DUMMIES = 8
-LEAD = [2,0,2,1,2,2,1,1,1,1,0,1,0,0,0,0]
+DUMMIES = 4
+LEAD = [1,1,1,1,2,2,0,1,2,1,0,2,0,0,0,0]
 HEAD_PAIRS = 2
-W2_HEAD = [4,1,0,4]
-W2_SLOT = [2,2,6,5,4,4,5,2,1,4,2,4,3,2,3,5]
-W2_TAIL = 1
-ON_SCALAR = []
+W2_HEAD = [3,2,0,1]
+W2_SLOT = [2,6,3,2,3,6,1,1,6,3,5,1,2,3,3,1]
+W2_TAIL = 3
+ON_SCALAR = [(6, 1), (0, 1)]
 LATE = []
 LATE_FIRST = 0
-LOADS = ["x0","v0","x1","v2","v1","x2","x3","v3","p0","w10","p1","p2","w11","p3","p5","p4","w21","w20"]
-MM_SLOT = [1,6,5,3,8,1,2,3,5,6,3,8,6,4,5,4]
-REL_BUFS = 3
+LOADS = ["x0","v1","v0","x1","v2","x2","x3","p0","v3","p1","w10","p2","w11","w20","p3","w21","p4","p5"]
+MM_SLOT = [7,2,5,4,2,3,7,4,5,2,2,7,5,4,4,8]
+REL_BUFS = 6
+BLOCK = 2
+V_SQ = []
+V_RELU = [[6,1],[7,1]]
+END = [2,0,0]
+TAIL_MM = 10
+OUT_PAR = 0
 W1C_BUFS = 10
-SQ_LAG = 2
+SQ_LAG = 4
 
 
 def tile_mlp_kernel(tc, x, W1, W2_bytes, W2_scale, out):
@@ -150,21 +156,23 @@ def tile_mlp_kernel(tc, x, W1, W2_bytes, W2_scale, out):
                     )
 
         def relu(m, h):
-            q, t = m // 2, 2 * (m % 2)
-            if t == 0 and h == 0:
-                rel[q] = work.tile([P, 4, 512], F32, name="rel", tag="rel", bufs=REL_BUFS)
-            nc.scalar.activation(
-                out=rel[q][:, t : t + 2, h * 256 : (h + 1) * 256],
-                in_=p1[m, h][:].rearrange("p (t n) -> p t n", t=2), func=AF.Relu,
-            )
+            q = m // 2
+            if (q, h) not in rel:
+                rel[q, h] = work.tile([P, 2, 256, 2], F32, name="rel", tag="rel", bufs=REL_BUFS)
+            dst, src = rel[q, h][:, m % 2, :, :], p1[m, h][:].rearrange("p (e n) -> p n e", e=2)
+            if (m, h) in V_RELU:
+                nc.vector.tensor_scalar(out=dst, in0=src, scalar1=0.0, scalar2=None, op0=ALU.max)
+            else:
+                nc.scalar.activation(out=dst, in_=src, func=AF.Relu)
 
         def square(q, h):
             pg[q, h] = work.tile([P, 1024], BF16, name="pg", tag="pg", bufs=4, align_bytes=64)
-            nc.scalar.activation(
-                out=pg[q, h][:].rearrange("p (c i t) -> p c t i", i=4, t=4),
-                in_=rel[q][:, :, h * 256 : (h + 1) * 256].rearrange("p t (c i) -> p c t i", i=4),
-                func=AF.Square,
-            )
+            dst = pg[q, h][:].rearrange("p (n r e) -> p n r e", r=2, e=2)
+            src = rel[q, h][:].rearrange("p r n e -> p n r e")
+            if (q, h) in V_SQ:
+                nc.vector.tensor_tensor(out=dst, in0=src, in1=src, op=ALU.mult)
+            else:
+                nc.scalar.activation(out=dst, in_=src, func=AF.Square)
 
         def quant_post(q, h):
             if h == 0:
@@ -291,12 +299,14 @@ def tile_mlp_kernel(tc, x, W1, W2_bytes, W2_scale, out):
             quant_w1(j)
 
         units = []
-        for q in range(N_PASS):
-            if q < N_PASS - 1:
-                units += [(2 * q, 0), (2 * q, 1), (2 * q + 1, 0), (2 * q + 1, 1)]
-            else:
-                units += [(2 * q, 0), (2 * q + 1, 0), (2 * q, 1), (2 * q + 1, 1)]
-        squares = [(q, h) for q in range(N_PASS) for h in range(2)]
+        squares = []
+        for q in range(N_PASS - BLOCK):
+            units += [(2 * q, 0), (2 * q, 1), (2 * q + 1, 0), (2 * q + 1, 1)]
+            squares += [(q, 0), (q, 1)]
+        for h in range(2):
+            for q in range(N_PASS - BLOCK, N_PASS):
+                units += [(2 * q, h), (2 * q + 1, h)]
+                squares += [(q, h)]
         post_at = {}
         w2_at = {}
         nxt = {}
@@ -385,24 +395,25 @@ def tile_mlp_kernel(tc, x, W1, W2_bytes, W2_scale, out):
                 square(*squares[m - SQ_LAG])
         rest = [squares[N_PAIRS - SQ_LAG + i] for i in range(SQ_LAG)]
         m = N_PAIRS
-        cap[0] = len(stream) if LATE_FIRST >= len(LATE) else cap[0]
-        for t in LATE[:LATE_FIRST]:
-            widen(N_PASS - 1, t)
+        cap[0] = len(stream)
         w2_run(m, W2_TAIL)
+        n_out = [0]
+
+        def drain():
+            for i, half in order[n_out[0] :]:
+                finish(n_out[0], i, half, n_out[0] % 2 == OUT_PAR)
+                n_out[0] += 1
+
         for n in range(SQ_LAG + 1):
             if n < SQ_LAG:
                 square(*rest[n])
-                if n == 0:
-                    cap[0] = len(stream)
-                    for t in LATE[LATE_FIRST:]:
-                        widen(N_PASS - 1, t)
             post(m)
-            run_mm(picks(m, 7))
-            w2_run(m, 2)
+            drain()
+            run_mm(picks(m, TAIL_MM))
+            w2_run(m, END[0])
             m += 1
         w2_run(m, 60)
         m += 1
         run_mm(picks(m, 64))
         assert len(order) == 8, nxt
-        for n, (i, half) in enumerate(order):
-            finish(n, i, half, n % 2 == 0)
+        drain()

@@ -19,22 +19,22 @@ P = 128
 N_PAIRS = 16
 N_PASS = 8
 DUMMIES = 4
-LEAD = [1,1,1,1,2,2,0,1,2,1,0,2,0,0,0,0]
+LEAD = [1,2,0,2,0,0,2,1,2,2,0,2,0,0,0,0]
 HEAD_PAIRS = 2
-W2_HEAD = [3,2,0,1]
-W2_SLOT = [2,6,3,2,3,6,1,1,6,3,5,1,2,3,3,1]
+W2_HEAD = [3,2,0,2]
+W2_SLOT = [5,4,2,2,4,2,1,2,6,4,2,4,2,3,3,1]
 W2_TAIL = 3
-ON_SCALAR = [(6, 1), (0, 1)]
+ON_SCALAR = [(6, 1)]
 LATE = []
 LATE_FIRST = 0
-LOADS = ["x0","v1","v0","x1","v2","x2","x3","p0","v3","p1","w10","p2","w11","w20","p3","w21","p4","p5"]
-MM_SLOT = [7,2,5,4,2,3,7,4,5,2,2,7,5,4,4,8]
+LOADS = ["x0","v0","x1","v2","x2","v1","x3","v3","p0","w10","p1","w11","p2","w21","p3","p4","w20","p5"]
+MM_SLOT = [2,4,4,8,4,6,2,4,8,4,5,6,4,3,4,6]
 REL_BUFS = 6
 BLOCK = 2
 V_SQ = []
-V_RELU = [[6,1],[7,1]]
+V_RELU = []
 END = [2,0,0]
-TAIL_MM = 10
+TAIL_MM = 16
 OUT_PAR = 0
 W1C_BUFS = 10
 SQ_LAG = 4
@@ -191,8 +191,9 @@ def tile_mlp_kernel(tc, x, W1, W2_bytes, W2_scale, out):
 
         def interleave(q, h):
             w2g[q, h] = work.tile([P, 2048], BF16, name="w2g", tag="w2g", bufs=3, align_bytes=64)
-            dst = w2g[q, h][:].rearrange("p (n r e) -> p n r e", r=2, e=2)
-            src = wide[q][:, :, h * 512 : (h + 1) * 512, :].rearrange("p r n e -> p n r e")
+            dst = w2g[q, h][:].bitcast(F32).rearrange("p (n r) -> p n r", r=2)
+            words = wide[q][:].rearrange("p r n e -> p r (n e)").bitcast(F32)
+            src = words[:, :, h * 512 : (h + 1) * 512].rearrange("p r n -> p n r")
             if (q, h) in ON_SCALAR:
                 nc.scalar.copy(out=dst, in_=src)
             else:

from contextlib import ExitStack

import concourse.mybir as mybir
from concourse.masks import make_identity

TOK, DIM, HID = 512, 1024, 4096
FLOPS = 2 * 2 * TOK * DIM * HID

F32 = mybir.dt.float32
BF16 = mybir.dt.bfloat16
U32 = mybir.dt.uint32
U8 = mybir.dt.uint8
FP8 = mybir.dt.float8_e4m3fn
FP8X4 = mybir.dt.float8_e4m3fn_x4
AF = mybir.ActivationFunctionType
ALU = mybir.AluOpType

P = 128
N_PAIRS = 16
N_PASS = 8
DUMMIES = 4
LEAD = [1,2,0,2,0,0,2,1,2,2,0,2,0,0,0,0]
HEAD_PAIRS = 2
W2_HEAD = [3,2,0,2]
W2_SLOT = [5,4,2,2,4,2,1,2,6,4,2,4,2,3,3,1]
W2_TAIL = 3
ON_SCALAR = [(6, 1)]
LATE = []
LATE_FIRST = 0
LOADS = ["x0","v0","x1","v2","x2","v1","x3","v3","p0","w10","p1","w11","p2","w21","p3","p4","w20","p5"]
MM_SLOT = [2,4,4,8,4,6,2,4,8,4,5,6,4,3,4,6]
REL_BUFS = 6
BLOCK = 2
V_SQ = []
V_RELU = []
END = [2,0,0]
TAIL_MM = 16
OUT_PAR = 0
W1C_BUFS = 10
SQ_LAG = 4


def tile_mlp_kernel(tc, x, W1, W2_bytes, W2_scale, out):
    nc = tc.nc
    x_v = x.rearrange("b s k -> (b s) k").rearrange("(p i) k -> p i k", i=4)
    w1_v = W1.rearrange("(a m t) k -> a m t k", m=P, t=4)
    w2_v = W2_bytes.rearrange("(a p t) d -> a p t d", p=P, t=4)
    sc_v = W2_scale.rearrange("(a p t) o -> p a (t o)", p=P, t=4)
    out_v = out.rearrange("b s d -> (b s) d").rearrange("(p i) d -> p i d", i=4)

    with ExitStack() as ctx:
        keep = ctx.enter_context(tc.tile_pool(name="keep", bufs=1))
        work = ctx.enter_context(tc.tile_pool(name="work", bufs=2))
        psum = ctx.enter_context(tc.psum_pool(name="psum", bufs=1))

        ident = keep.tile([P, P], F32, name="ident")
        zeros = keep.tile([P, 512], BF16, name="zeros")
        probe = keep.tile([P, 1], F32, name="probe")
        probe2 = keep.tile([P, 1], F32, name="probe2")
        scale = keep.tile([P, N_PASS, 4], F32, name="scale")
        xg = [keep.tile([P, 2048], BF16, name="xg%d" % n, align_bytes=64) for n in range(2)]
        xc = keep.tile([P, 1024], U32, name="xc", align_bytes=64)
        xs = keep.tile([P, 1024], U8, name="xs", align_bytes=64)

        ctx.enter_context(tc.manual_schedule())

        raw = {}
        bytes_t = {}
        wide = {}
        w2g = {}
        w2c = {}
        w2s = {}
        wg = {}
        w1c = {}
        w1s = {}
        rel = {}
        pg = {}
        pc = {}
        ps = {}
        tp = {}
        p1 = {}
        acc = {}
        n_unit = [0]

        def bank(tag):
            return psum.tile([P, 512], F32, name="bk_" + tag, tag=tag)

        def load_x(i):
            raw["x", i] = work.tile([P, 1024], BF16, name="xraw", tag="xraw", bufs=4)
            nc.sync.dma_start(out=raw["x", i][:], in_=x_v[:, i, :])

        def load_w1(j):
            t = work.tile([P, 2, 1024], BF16, name="w1raw", tag="w1raw", bufs=6)
            nc.sync.dma_start(out=t[:], in_=w1_v[j // 2][:, 2 * (j % 2) : 2 * (j % 2) + 2, :])
            raw["w", 2 * j] = t[:, 0, :]
            raw["w", 2 * j + 1] = t[:, 1, :]

        def load_w2(q, h):
            t = work.tile([P, 2, 1024], U8, name="w2b", tag="w2b", bufs=6)
            nc.sync.dma_start(out=t[:], in_=w2_v[q][:, 2 * h : 2 * h + 2, :])
            bytes_t[q, 2 * h] = t[:, 0, :]
            bytes_t[q, 2 * h + 1] = t[:, 1, :]

        def load_w2_row(q, t):
            b = keep.tile([P, 1024], U8, name="w2r%d" % t)
            nc.sync.dma_start(out=b[:], in_=w2_v[q][:, t, :])
            bytes_t[q, t] = b[:]

        def transposes(kind, n, b):
            src = raw[kind, n]
            words = (src[:] if kind == "x" else src).bitcast(F32)
            t = bank("tp%d" % b)
            tp[kind, n] = t
            for g in range(2):
                for u in range(2):
                    nc.tensor.transpose(
                        t[:, (2 * g + u) * P : (2 * g + u + 1) * P],
                        words[:, 256 * g + u : 256 * (g + 1) : 2],
                        ident[:],
                    )

        def evac(kind, n):
            src = tp[kind, n][:].rearrange("p (g u m) -> p g m u", g=2, u=2)
            if kind == "x":
                dst = xg[n // 2][:].bitcast(F32).rearrange("p (g i m u) -> p g i m u", g=2, i=2, u=2)[:, :, n % 2]
            else:
                if n % 2 == 0:
                    wg[n // 2] = work.tile([P, 2048], BF16, name="wg", tag="wg", bufs=4, align_bytes=64)
                h = n % 2
                dst = wg[n // 2][:, h * 1024 : (h + 1) * 1024].bitcast(F32).rearrange("p (g m u) -> p g m u", g=2, u=2)
            nc.scalar.copy(out=dst, in_=src)

        def quant_x(ip, g):
            o = slice(g * 512 + ip * 256, g * 512 + ip * 256 + 256)
            nc.vector.quantize_mx(
                out=xc[:, o].bitcast(FP8X4), scales=xs[:, o],
                in_=xg[ip][:, g * 1024 : (g + 1) * 1024],
            )

        def quant_w1(j):
            w1c[j] = work.tile([P, 512], U32, name="w1c", tag="w1c", bufs=W1C_BUFS, align_bytes=64)
            w1s[j] = work.tile([P, 512], U8, name="w1s", tag="w1s", bufs=W1C_BUFS, align_bytes=64)
            nc.vector.quantize_mx(out=w1c[j][:].bitcast(FP8X4), scales=w1s[j][:], in_=wg[j][:])

        def mm1(m, h):
            t = bank("p1%d" % (n_unit[0] % 2))
            n_unit[0] += 1
            p1[m, h] = t
            for s in range(2):
                for g in range(2):
                    c = slice((2 * s + g) * P, (2 * s + g + 1) * P)
                    r = slice(g * 512 + h * 256, g * 512 + h * 256 + 256)
                    nc.tensor.matmul_mx(
                        out=t[:, s * 256 : (s + 1) * 256], lhsT=w1c[m][:, c].bitcast(FP8X4), lhsT_scale=w1s[m][:, c],
                        rhs=xc[:, r].bitcast(FP8X4), rhs_scale=xs[:, r], start=(g == 0), stop=(g == 1),
                    )

        def relu(m, h):
            q = m // 2
            if (q, h) not in rel:
                rel[q, h] = work.tile([P, 2, 256, 2], F32, name="rel", tag="rel", bufs=REL_BUFS)
            dst, src = rel[q, h][:, m % 2, :, :], p1[m, h][:].rearrange("p (e n) -> p n e", e=2)
            if (m, h) in V_RELU:
                nc.vector.tensor_scalar(out=dst, in0=src, scalar1=0.0, scalar2=None, op0=ALU.max)
            else:
                nc.scalar.activation(out=dst, in_=src, func=AF.Relu)

        def square(q, h):
            pg[q, h] = work.tile([P, 1024], BF16, name="pg", tag="pg", bufs=4, align_bytes=64)
            dst = pg[q, h][:].rearrange("p (n r e) -> p n r e", r=2, e=2)
            src = rel[q, h][:].rearrange("p r n e -> p n r e")
            if (q, h) in V_SQ:
                nc.vector.tensor_tensor(out=dst, in0=src, in1=src, op=ALU.mult)
            else:
                nc.scalar.activation(out=dst, in_=src, func=AF.Square)

        def quant_post(q, h):
            if h == 0:
                pc[q] = keep.tile([P, 512], U32, name="pc%d" % q, align_bytes=64)
                ps[q] = keep.tile([P, 512], U8, name="ps%d" % q, align_bytes=64)
            o = slice(h * 256, (h + 1) * 256)
            nc.vector.quantize_mx(out=pc[q][:, o].bitcast(FP8X4), scales=ps[q][:, o], in_=pg[q, h][:])

        def widen(q, t):
            if q not in wide:
                wide[q] = work.tile([P, 2, 1024, 2], BF16, name="wide", tag="wide", bufs=2)
            src = bytes_t[q, t].bitcast(FP8)
            nc.vector.tensor_scalar(
                out=wide[q][:, t // 2, :, t % 2], in0=src, scalar1=scale[:, q, t : t + 1], scalar2=None, op0=ALU.mult
            )

        def interleave(q, h):
            w2g[q, h] = work.tile([P, 2048], BF16, name="w2g", tag="w2g", bufs=3, align_bytes=64)
            dst = w2g[q, h][:].bitcast(F32).rearrange("p (n r) -> p n r", r=2)
            words = wide[q][:].rearrange("p r n e -> p r (n e)").bitcast(F32)
            src = words[:, :, h * 512 : (h + 1) * 512].rearrange("p r n -> p n r")
            if (q, h) in ON_SCALAR:
                nc.scalar.copy(out=dst, in_=src)
            else:
                nc.vector.tensor_copy(out=dst, in_=src)

        def quant_w2(q, h):
            if h == 0:
                w2c[q] = keep.tile([P, 1024], U32, name="w2c%d" % q, align_bytes=64)
                w2s[q] = keep.tile([P, 1024], U8, name="w2s%d" % q, align_bytes=64)
            o = slice(h * 512, (h + 1) * 512)
            nc.vector.quantize_mx(out=w2c[q][:, o].bitcast(FP8X4), scales=w2s[q][:, o], in_=w2g[q, h][:])

        stream = [("widen", 0, t) for t in (0, 2, 1, 3)]
        for q in range(N_PASS):
            nxt = [("widen", q + 1, t) if q + 1 < N_PASS else None for t in (0, 2, 1, 3)]
            tail = [("interleave", q, 0), ("quant", q, 0), ("interleave", q, 1), ("quant", q, 1)]
            for a, b in zip(nxt, tail):
                if a:
                    stream.append(a)
                stream.append(b)
        pos = [0]
        cap = [stream.index(("interleave", N_PASS - 1, 0))]

        def w2_work(n):
            n = min(n, cap[0] - pos[0])
            for kind, q, a in stream[pos[0] : pos[0] + n]:
                if kind == "widen":
                    widen(q, a)
                    if a in (1, 3) and q + 3 < N_PASS:
                        load_w2(q + 3, a // 2)
                elif kind == "interleave":
                    interleave(q, a)
                else:
                    quant_w2(q, a)
            pos[0] += n

        tags = {(0, 1): "tp0", (1, 1): "tp1", (2, 1): "p10", (3, 1): "p11"}

        def mm2(i, half, q):
            if q == 0:
                acc[i, half] = bank(tags.get((i, half), "acc%d" % i))
            c = slice(i * P, (i + 1) * P)
            r = slice(half * 512, (half + 1) * 512)
            nc.tensor.matmul_mx(
                out=acc[i, half][:], lhsT=pc[q][:, c].bitcast(FP8X4), lhsT_scale=ps[q][:, c],
                rhs=w2c[q][:, r].bitcast(FP8X4), rhs_scale=w2s[q][:, r],
                start=(q == 0), stop=(q == N_PASS - 1),
            )

        def finish(n, i, half, on_scalar):
            tag, bufs = ("w1raw", 6) if n < 6 else ("wide", 2)
            o = work.tile([P, 512], F32, name="o", tag=tag, bufs=bufs)
            if on_scalar:
                nc.scalar.copy(out=o[:], in_=acc[i, half][:])
            else:
                nc.vector.tensor_copy(out=o[:], in_=acc[i, half][:])
            nc.sync.dma_start(out=out_v[:, i, half * 512 : (half + 1) * 512], in_=o[:])

        nc.vector.memset(zeros[:], 0.0)
        nc.vector.memset(probe[:], 0.0)
        make_identity(nc, ident[:])
        nc.scalar.dma_start(out=scale[:], in_=sc_v)
        nc.scalar.activation(out=probe2[:], in_=probe[:], func=AF.Square)
        for code in LOADS:
            if code[0] == "x":
                load_x(int(code[1]))
            elif code[0] == "p":
                load_w1(int(code[1]))
            elif code[0] == "v":
                load_w2_row(0, int(code[1]))
            else:
                load_w2(int(code[1]), int(code[2]))

        warm = bank("acc3")
        for d in range(DUMMIES):
            nc.tensor.matmul(warm[:], lhsT=zeros[:, :P], rhs=zeros[:], start=True, stop=True)

        w2_work(W2_HEAD[0])
        for ip in range(2):
            for i in (2 * ip, 2 * ip + 1):
                transposes("x", i, i % 2)
            for i in (2 * ip, 2 * ip + 1):
                evac("x", i)
            for g in range(2):
                quant_x(ip, g)
        w2_work(W2_HEAD[1])

        n_t = [0]

        def tpair():
            j = n_t[0]
            for s in range(2):
                transposes("w", 2 * j + s, s)
            if j + 6 < N_PAIRS:
                load_w1(j + 6)
            for s in range(2):
                evac("w", 2 * j + s)
            n_t[0] += 1
            return j

        for n in range(HEAD_PAIRS):
            j = tpair()
            w2_work(W2_HEAD[2 + n])
            quant_w1(j)

        units = []
        squares = []
        for q in range(N_PASS - BLOCK):
            units += [(2 * q, 0), (2 * q, 1), (2 * q + 1, 0), (2 * q + 1, 1)]
            squares += [(q, 0), (q, 1)]
        for h in range(2):
            for q in range(N_PASS - BLOCK, N_PASS):
                units += [(2 * q, h), (2 * q + 1, h)]
                squares += [(q, h)]
        post_at = {}
        w2_at = {}
        nxt = {}
        accs = [(0, 0), (1, 0), (2, 0), (3, 0), (0, 1), (1, 1), (2, 1), (3, 1)]

        def picks(m, limit):
            res = []
            more = True
            while more and len(res) < limit:
                more = False
                for a in accs:
                    i, half = a
                    q = nxt.get(a, 0)
                    if q == N_PASS or len(res) == limit:
                        continue
                    if half == 1 and i < 2 and n_t[0] < N_PAIRS:
                        continue
                    if half == 1 and i >= 2 and m < N_PAIRS:
                        continue
                    if m > post_at.get((q, i // 2), 999) and m > w2_at.get((q, half), 999):
                        res.append((i, half, q))
                        nxt[a] = q + 1
                        more = True
            return res

        order = []

        def run_mm(lst):
            for i, half, q in lst:
                mm2(i, half, q)
                if q == N_PASS - 1:
                    order.append((i, half))

        def w2_run(m, n):
            n = min(n, cap[0] - pos[0])
            for kind, q, a in stream[pos[0] : pos[0] + n]:
                if kind == "quant":
                    w2_at[q, a] = m
            w2_work(n)

        for kind, q, a in stream[: pos[0]]:
            if kind == "quant":
                w2_at[q, a] = -1

        def post(m):
            if 0 <= m - SQ_LAG - 1 < 2 * N_PASS:
                k = squares[m - SQ_LAG - 1]
                quant_post(*k)
                post_at[k] = m

        for m in range(N_PAIRS):
            passes = picks(m, MM_SLOT[m])
            ua, ub = units[2 * m], units[2 * m + 1]
            n2 = W2_SLOT[m]
            if LEAD[m]:
                j = tpair()
                w2_run(m, n2 // 2)
                post(m)
                quant_w1(j)
                mm1(*ua)
                mm1(*ub)
                relu(*ua)
                relu(*ub)
                if LEAD[m] == 1:
                    run_mm(passes)
                for r in range(LEAD[m] - 1):
                    j = tpair()
                    if r == 0:
                        w2_run(m, n2 - n2 // 2)
                    quant_w1(j)
                    if r == 0:
                        run_mm(passes)
                if LEAD[m] == 1:
                    w2_run(m, n2 - n2 // 2)
            else:
                mm1(*ua)
                run_mm(passes[:2])
                mm1(*ub)
                run_mm(passes[2:])
                relu(*ua)
                relu(*ub)
                w2_run(m, 1)
                post(m)
                w2_run(m, n2 - 1)
            if SQ_LAG <= m:
                square(*squares[m - SQ_LAG])
        rest = [squares[N_PAIRS - SQ_LAG + i] for i in range(SQ_LAG)]
        m = N_PAIRS
        cap[0] = len(stream)
        w2_run(m, W2_TAIL)
        n_out = [0]

        def drain():
            for i, half in order[n_out[0] :]:
                finish(n_out[0], i, half, n_out[0] % 2 == OUT_PAR)
                n_out[0] += 1

        for n in range(SQ_LAG + 1):
            if n < SQ_LAG:
                square(*rest[n])
            post(m)
            drain()
            run_mm(picks(m, TAIL_MM))
            w2_run(m, END[0])
            m += 1
        w2_run(m, 60)
        m += 1
        run_mm(picks(m, 64))
        assert len(order) == 8, nxt
        drain()
